import numpy as np
import ml_dtypes


def mxq(x, axis, fmt="e4m3"):
    dtype, down = {"e4m3": (ml_dtypes.float8_e4m3fn, 7), "e5m2": (ml_dtypes.float8_e5m2, 14)}[fmt]
    v = np.moveaxis(np.asarray(x, np.float32).astype(ml_dtypes.bfloat16).astype(np.float64), axis, -1)
    blocks = v.reshape(v.shape[:-1] + (-1, 32))
    amax = np.abs(blocks).max(-1, keepdims=True)
    byte = np.maximum(np.where(amax > 0, np.frexp(amax)[1] - 1 + 127, 0) - down, 1)
    scale = np.exp2(byte - 127.0)
    codes = (blocks / scale).astype(np.float32).astype(dtype).astype(np.float64)
    return np.moveaxis((codes * scale).reshape(v.shape), -1, axis)


WIDE = False


def mx_kscale(k):
    if not WIDE:
        return np.ones(k)
    levels = np.array([10, -10, 5, -5, 0])
    a = np.random.permutation(np.resize(levels, k // 512 * 4)).reshape(k // 512, 4)
    idx = np.arange(k)
    return np.exp2(a[idx // 512, idx % 128 // 32])


BF16 = ml_dtypes.bfloat16


def bf(x):
    return np.asarray(x, np.float32).astype(BF16)


def f64(x):
    return np.asarray(x).astype(np.float64)


B, H, T, D, W = 1, 4, 4096, 128, 512
NB = T // W
C0 = 4.0


def band(i, j):
    return (j[None, :] <= i[:, None]) & ((i[:, None] - j[None, :]) < W)


def lead(x, fill):
    return np.concatenate([np.full_like(x[:, :, :1], fill), x], axis=2)


def setup_inputs():
    s = mx_kscale(W)
    s = np.tile(np.roll(s, -np.argmax(s)), NB)
    q = np.random.standard_normal((B, H, T, D)) * 1.5
    k = np.random.standard_normal((B, H, T, D))
    v = np.random.standard_normal((B, H, T, D)) * 2.0
    q[..., 0] = C0
    k[..., 0] += np.log(s) * D ** 0.5 / C0
    v = v * (s.max() / s)[:, None]
    return {"q": bf(q), "k": bf(k), "v": bf(v)}


def reference(q, k, v):
    a = np.arange(W)
    qb = f64(q).reshape(B, H, NB, W, D)
    kb = f64(k).reshape(B, H, NB, W, D)
    vq = mxq(f64(v).reshape(B, H, NB, W, D), 3, "e4m3")
    s0 = np.where(band(a, a), qb @ kb.swapaxes(-1, -2) * D ** -0.5, -np.inf)
    s1 = np.where(band(a + W, a), qb[:, :, 1:] @ kb[:, :, :-1].swapaxes(-1, -2) * D ** -0.5, -np.inf)
    m = np.maximum(s0.max(-1, keepdims=True), lead(s1.max(-1, keepdims=True), -np.inf))
    e0 = np.exp(s0 - m)
    e1 = np.exp(s1 - m[:, :, 1:])
    num = (mxq(e0, 4, "e4m3") @ vq) + lead(mxq(e1, 4, "e4m3") @ vq[:, :, :-1], 0.0)
    den = e0.sum(-1, keepdims=True) + lead(e1.sum(-1, keepdims=True), 0.0)
    return (num / den).reshape(B, H, T, D)

@@ -1,0 +1,192 @@
+from contextlib import ExitStack
+
+import concourse.mybir as mybir
+from concourse.masks import make_identity
+
+F32 = mybir.dt.float32
+BF16 = mybir.dt.bfloat16
+U32 = mybir.dt.uint32
+U8 = mybir.dt.uint8
+FP8X4 = mybir.dt.float8_e4m3fn_x4
+ALU = mybir.AluOpType
+ACTF = mybir.ActivationFunctionType
+AX = mybir.AxisListType
+
+P = 128
+H = 4
+T = 4096
+W = 512
+NB = T // W
+SUBS = W // P
+SCALE = 128.0 ** -0.5
+NEG = -(2.0 ** 80)
+FLOPS = 2 * (2 * NB - 1) * H * 2 * W * W * P
+
+
+def tile_baseattention_t_kernel(tc, q, k, v, out):
+    nc = tc.nc
+    qv = q.rearrange("b h (s p) d -> p (b h s) d", p=P)
+    kv = k.rearrange("b h (s p) d -> p (b h s) d", p=P)
+    vv = v.rearrange("b h (s p) d -> p (b h s) d", p=P)
+    ov = out.rearrange("b h (s p) d -> p (b h s) d", p=P)
+    NS = T // P
+
+    with ExitStack() as ctx:
+        const = ctx.enter_context(tc.tile_pool(name="const", bufs=1))
+        stat = ctx.enter_context(tc.tile_pool(name="stat", bufs=6))
+        ep = ctx.enter_context(tc.tile_pool(name="ep", bufs=3))
+        wp = ctx.enter_context(tc.tile_pool(name="wp", bufs=3))
+        vgp = ctx.enter_context(tc.tile_pool(name="vgp", bufs=2))
+        op = ctx.enter_context(tc.tile_pool(name="op", bufs=3))
+        ps_s = ctx.enter_context(tc.psum_pool(name="ps_s", bufs=2))
+        ps_t = ctx.enter_context(tc.psum_pool(name="ps_t", bufs=2))
+        ps_o = ctx.enter_context(tc.psum_pool(name="ps_o", bufs=1))
+        ps_p = ctx.enter_context(tc.psum_pool(name="ps_p", bufs=1))
+
+        q_raw = []
+        k_raw = []
+        v_raw = []
+        for h in range(H):
+            q_raw.append(const.tile([P, NS, P], BF16, name="q_raw%d" % h))
+            k_raw.append(const.tile([P, NS, P], BF16, name="k_raw%d" % h))
+            v_raw.append(const.tile([P, NS, P], BF16, name="v_raw%d" % h))
+        for h in range(H):
+            cuts = [0, 8, NS] if h == 0 else [0, NS]
+            for c in range(len(cuts) - 1):
+                a, b = cuts[c], cuts[c + 1]
+                nc.sync.dma_start(out=q_raw[h][:, a:b, :], in_=qv[:, h * NS + a:h * NS + b, :])
+                nc.sync.dma_start(out=k_raw[h][:, a:b, :], in_=kv[:, h * NS + a:h * NS + b, :])
+                nc.sync.dma_start(out=v_raw[h][:, a:b, :], in_=vv[:, h * NS + a:h * NS + b, :])
+
+        ident = const.tile([P, P], BF16, name="ident")
+        make_identity(nc, ident[:])
+        mask_f = const.tile([P, 2, P], F32, name="mask_f")
+        nc.gpsimd.memset(mask_f[:], 0.0)
+        nc.gpsimd.affine_select(out=mask_f[:, 0, :], in_=mask_f[:, 0, :], compare_op=ALU.is_ge, fill=NEG,
+                                base=-1, pattern=[[1, P]], channel_multiplier=-1)
+        nc.gpsimd.affine_select(out=mask_f[:, 1, :], in_=mask_f[:, 1, :], compare_op=ALU.is_ge, fill=NEG,
+                                base=0, pattern=[[-1, P]], channel_multiplier=1)
+        mask = const.tile([P, 2, P], BF16, name="mask")
+        nc.vector.tensor_copy(out=mask[:], in_=mask_f[:])
+
+        grouped = []
+        for j in range(SUBS):
+            g = const.tile([P, 2, P, 4], BF16, name="grouped%d" % j, align_bytes=64)
+            nc.vector.memset(g[:].rearrange("p a q t -> p (a q t)"), 0.0)
+            grouped.append(g)
+
+        xT = []
+        v_words = []
+        v_scales = []
+        for h in range(H):
+            xT.append(const.tile([P, 2, T], BF16, name="xT%d" % h))
+            v_words.append(const.tile([P, NB, P], U32, name="v_words%d" % h, align_bytes=64))
+            v_scales.append(const.tile([P, NB, P], U8, name="v_scales%d" % h, align_bytes=64))
+
+        def prep(h, n):
+            p_ps = ps_p.tile([P, 2 * SUBS, P], BF16)
+            for j in range(SUBS):
+                nc.tensor.transpose(p_ps[:, j, :], q_raw[h][:, n * SUBS + j, :], ident[:])
+            for j in range(SUBS):
+                nc.tensor.transpose(p_ps[:, SUBS + j, :], k_raw[h][:, n * SUBS + j, :], ident[:])
+            nc.vector.tensor_copy(out=xT[h][:, :, n * W:(n + 1) * W],
+                                  in_=p_ps[:].rearrange("p (a j) c -> p a (j c)", a=2))
+            v_g = vgp.tile([P, P, 4], BF16, align_bytes=64)
+            nc.vector.tensor_copy(out=v_g[:], in_=v_raw[h][:, n * SUBS:(n + 1) * SUBS, :].rearrange("p t d -> p d t"))
+            nc.vector.quantize_mx(out=v_words[h][:, n, :].bitcast(FP8X4), scales=v_scales[h][:, n, :],
+                                  in_=v_g[:].rearrange("p d t -> p (d t)"))
+
+        state = {}
+
+        def scores(i, h, n, qt):
+            s_ps = ps_s.tile([P, 2 * W], F32)
+            row = n * SUBS + qt
+            qT = xT[h][:, 0, row * P:(row + 1) * P]
+            k0 = (row - SUBS) * P
+            first = 0 if n > 0 else SUBS - qt
+            if n > 0:
+                nc.tensor.matmul(s_ps[:, 0:P], lhsT=ident[:], rhs=mask[:, 0, :], start=True, stop=False)
+            nc.tensor.matmul(s_ps[:, W:W + P], lhsT=ident[:], rhs=mask[:, 1, :], start=True, stop=False)
+            if n > 0:
+                nc.tensor.matmul(s_ps[:, 0:P], lhsT=qT, rhs=xT[h][:, 1, k0:k0 + P], start=False, stop=True)
+            lo = 1 if n > 0 else first
+            if lo < SUBS:
+                nc.tensor.matmul(s_ps[:, lo * P:W], lhsT=qT, rhs=xT[h][:, 1, k0 + lo * P:k0 + W], start=True, stop=True)
+            nc.tensor.matmul(s_ps[:, W:W + P], lhsT=qT, rhs=xT[h][:, 1, k0 + W:k0 + W + P], start=False, stop=True)
+            mm = stat.tile([P, 2], F32)
+            nm = stat.tile([P, 1], F32)
+            nc.vector.tensor_reduce(out=mm[:, 1:2], in_=s_ps[:, W:W + P], axis=AX.X, op=ALU.max)
+            if first < SUBS:
+                nc.vector.tensor_reduce(out=mm[:, 0:1], in_=s_ps[:, first * P:W], axis=AX.X, op=ALU.max)
+                nc.vector.tensor_scalar(out=nm[:], in0=mm[:, 0:1], scalar1=mm[:, 1:2], scalar2=-SCALE,
+                                        op0=ALU.max, op1=ALU.mult)
+            else:
+                nc.vector.tensor_scalar(out=nm[:], in0=mm[:, 1:2], scalar1=-SCALE, scalar2=None, op0=ALU.mult)
+            e_sb = ep.tile([P, 5 * P], BF16)
+            dn = stat.tile([P, 2], F32)
+            if first < SUBS:
+                nc.scalar.activation(out=e_sb[:, first * P:W], in_=s_ps[:, first * P:W], func=ACTF.Exp,
+                                     bias=nm[:], scale=SCALE, accum_out=dn[:, 0:1])
+            nc.scalar.activation(out=e_sb[:, W:W + P], in_=s_ps[:, W:W + P], func=ACTF.Exp,
+                                 bias=nm[:], scale=SCALE, accum_out=dn[:, 1:2])
+            state[i] = {"e": e_sb, "dn": dn, "first": first}
+
+        def flip(i, h, n, qt):
+            st = state[i]
+            first = st["first"]
+            e_sb = st["e"]
+            t_ps = ps_t.tile([P, 5, P], BF16)
+            for w in range(first, 5):
+                nc.tensor.transpose(t_ps[:, w, :], e_sb[:, w * P:(w + 1) * P], ident[:])
+            g = grouped[qt]
+            ra = SUBS - qt
+            if n > 0:
+                nc.scalar.copy(out=g[:, 0, :, qt:SUBS], in_=t_ps[:, 0:ra, :].rearrange("p t c -> p c t"))
+            nc.scalar.copy(out=g[:, 1, :, 0:qt + 1], in_=t_ps[:, ra:5, :].rearrange("p t c -> p c t"))
+
+        def finish(i, h, n, qt):
+            st = state[i]
+            g = grouped[qt]
+            e_words = wp.tile([P, 2 * P], U32, align_bytes=64)
+            e_scales = wp.tile([P, 2 * P], U8, align_bytes=64)
+            a0 = 0 if n > 0 else 1
+            nc.vector.quantize_mx(out=e_words[:, a0 * P:].bitcast(FP8X4), scales=e_scales[:, a0 * P:],
+                                  in_=g[:, a0:, :, :].rearrange("p a c t -> p (a c t)"))
+            o_ps = ps_o.tile([P, P], F32)
+            for a in range(a0, 2):
+                nc.tensor.matmul_mx(out=o_ps[:], lhsT=e_words[:, a * P:(a + 1) * P].bitcast(FP8X4),
+                                    lhsT_scale=e_scales[:, a * P:(a + 1) * P],
+                                    rhs=v_words[h][:, n - 1 + a, :].bitcast(FP8X4),
+                                    rhs_scale=v_scales[h][:, n - 1 + a, :],
+                                    start=(a == a0), stop=(a == 1))
+            dn = st["dn"]
+            rd = stat.tile([P, 1], F32)
+            if st["first"] < SUBS:
+                ds = stat.tile([P, 1], F32)
+                nc.vector.tensor_tensor(out=ds[:], in0=dn[:, 0:1], in1=dn[:, 1:2], op=ALU.add)
+                nc.vector.reciprocal(out=rd[:], in_=ds[:])
+            else:
+                nc.vector.reciprocal(out=rd[:], in_=dn[:, 1:2])
+            if qt == 0:
+                o_sb = op.tile([P, SUBS, P], F32)
+                state["o"] = o_sb
+            o_sb = state["o"]
+            nc.vector.tensor_scalar(out=o_sb[:, qt, :], in0=o_ps[:], scalar1=rd[:], scalar2=None, op0=ALU.mult)
+            if qt == SUBS - 1:
+                r0 = h * NS + n * SUBS
+                nc.sync.dma_start(out=ov[:, r0:r0 + SUBS, :], in_=o_sb[:])
+
+        tiles = [(h, n, qt) for h in range(H) for n in range(NB) for qt in range(SUBS)]
+        blocks = [(h, n) for h in range(H) for n in range(NB)]
+        NT = len(tiles)
+        prep(*blocks[0])
+        prep(*blocks[1])
+        for s in range(NT + 2):
+            if s < NT:
+                if s % SUBS == 1 and s // SUBS + 2 < len(blocks):
+                    prep(*blocks[s // SUBS + 2])
+                scores(s, *tiles[s])
+            if 0 <= s - 1 < NT:
+                flip(s - 1, *tiles[s - 1])
+            if 0 <= s - 2 < NT:
+                finish(s - 2, *tiles[s - 2])

@@ -18,9 +18,17 @@ T = 4096
 W = 512
 NB = T // W
 SUBS = W // P
+NS = T // P
 SCALE = 128.0 ** -0.5
 NEG = -(2.0 ** 80)
 FLOPS = 2 * (2 * NB - 1) * H * 2 * W * W * P
+
+L_MAX = 1
+L_EXP = 2
+L_FLIP = 3
+L_QUANT = 4
+L_MX = 5
+L_OUT = 6
 
 
 def tile_baseattention_t_kernel(tc, q, k, v, out):
@@ -29,19 +37,16 @@ def tile_baseattention_t_kernel(tc, q, k, v, out):
     kv = k.rearrange("b h (s p) d -> p (b h s) d", p=P)
     vv = v.rearrange("b h (s p) d -> p (b h s) d", p=P)
     ov = out.rearrange("b h (s p) d -> p (b h s) d", p=P)
-    NS = T // P
 
     with ExitStack() as ctx:
         const = ctx.enter_context(tc.tile_pool(name="const", bufs=1))
-        stat = ctx.enter_context(tc.tile_pool(name="stat", bufs=6))
+        stat = ctx.enter_context(tc.tile_pool(name="stat", bufs=4))
         ep = ctx.enter_context(tc.tile_pool(name="ep", bufs=3))
         wp = ctx.enter_context(tc.tile_pool(name="wp", bufs=3))
         vgp = ctx.enter_context(tc.tile_pool(name="vgp", bufs=2))
         op = ctx.enter_context(tc.tile_pool(name="op", bufs=3))
-        ps_s = ctx.enter_context(tc.psum_pool(name="ps_s", bufs=2))
-        ps_t = ctx.enter_context(tc.psum_pool(name="ps_t", bufs=2))
-        ps_o = ctx.enter_context(tc.psum_pool(name="ps_o", bufs=1))
-        ps_p = ctx.enter_context(tc.psum_pool(name="ps_p", bufs=1))
+        psum = ctx.enter_context(tc.psum_pool(name="psum", bufs=1))
+        ctx.enter_context(tc.manual_schedule())
 
         q_raw = []
         k_raw = []
@@ -50,29 +55,32 @@ def tile_baseattention_t_kernel(tc, q, k, v, out):
             q_raw.append(const.tile([P, NS, P], BF16, name="q_raw%d" % h))
             k_raw.append(const.tile([P, NS, P], BF16, name="k_raw%d" % h))
             v_raw.append(const.tile([P, NS, P], BF16, name="v_raw%d" % h))
-        for h in range(H):
-            cuts = [0, 8, NS] if h == 0 else [0, NS]
-            for c in range(len(cuts) - 1):
-                a, b = cuts[c], cuts[c + 1]
-                nc.sync.dma_start(out=q_raw[h][:, a:b, :], in_=qv[:, h * NS + a:h * NS + b, :])
-                nc.sync.dma_start(out=k_raw[h][:, a:b, :], in_=kv[:, h * NS + a:h * NS + b, :])
-                nc.sync.dma_start(out=v_raw[h][:, a:b, :], in_=vv[:, h * NS + a:h * NS + b, :])
+
+        def load(h, a, b):
+            nc.sync.dma_start(out=q_raw[h][:, a:b, :], in_=qv[:, h * NS + a:h * NS + b, :])
+            nc.sync.dma_start(out=k_raw[h][:, a:b, :], in_=kv[:, h * NS + a:h * NS + b, :])
+            nc.sync.dma_start(out=v_raw[h][:, a:b, :], in_=vv[:, h * NS + a:h * NS + b, :])
+
+        load(0, 0, 8)
+        load(0, 8, 16)
+        load(0, 16, NS)
 
         ident = const.tile([P, P], BF16, name="ident")
         make_identity(nc, ident[:])
-        mask_f = const.tile([P, 2, P], F32, name="mask_f")
-        nc.gpsimd.memset(mask_f[:], 0.0)
+        mask_f = const.tile([P, 3, P], F32, name="mask_f")
+        nc.gpsimd.memset(mask_f[:, 0:2, :], 0.0)
+        nc.gpsimd.memset(mask_f[:, 2, :], NEG)
         nc.gpsimd.affine_select(out=mask_f[:, 0, :], in_=mask_f[:, 0, :], compare_op=ALU.is_ge, fill=NEG,
                                 base=-1, pattern=[[1, P]], channel_multiplier=-1)
         nc.gpsimd.affine_select(out=mask_f[:, 1, :], in_=mask_f[:, 1, :], compare_op=ALU.is_ge, fill=NEG,
                                 base=0, pattern=[[-1, P]], channel_multiplier=1)
-        mask = const.tile([P, 2, P], BF16, name="mask")
+        mask = const.tile([P, 3, P], BF16, name="mask")
         nc.vector.tensor_copy(out=mask[:], in_=mask_f[:])
 
         grouped = []
         for j in range(SUBS):
             g = const.tile([P, 2, P, 4], BF16, name="grouped%d" % j, align_bytes=64)
-            nc.vector.memset(g[:].rearrange("p a q t -> p (a q t)"), 0.0)
+            nc.vector.memset(g[:].rearrange("p a c t -> p (a c t)"), 0.0)
             grouped.append(g)
 
         xT = []
@@ -83,110 +91,207 @@ def tile_baseattention_t_kernel(tc, q, k, v, out):
             v_words.append(const.tile([P, NB, P], U32, name="v_words%d" % h, align_bytes=64))
             v_scales.append(const.tile([P, NB, P], U8, name="v_scales%d" % h, align_bytes=64))
 
-        def prep(h, n):
-            p_ps = ps_p.tile([P, 2 * SUBS, P], BF16)
+        s_main = [psum.tile([P, W], F32, name="s_main%d" % j) for j in range(3)]
+        s_edge = [psum.tile([P, SUBS, P], F32, name="s_edge%d" % j) for j in range(2)]
+        flipped = [psum.tile([P, 2 * SUBS, P], BF16, name="flipped%d" % j) for j in range(2)]
+        o_ps = psum.tile([P, SUBS, P], F32, name="o_ps")
+
+        tiles = [(h, n, qt) for h in range(H) for n in range(NB) for qt in range(SUBS)]
+        blocks = [(h, n) for h in range(H) for n in range(NB)]
+        NT = len(tiles)
+        NBLK = len(blocks)
+        state = {}
+        bstate = {}
+        ring = {"flip": 0}
+
+        def next_flip():
+            j = ring["flip"]
+            ring["flip"] = 1 - j
+            return flipped[j]
+
+        def prep_pe(b):
+            h, n = blocks[b]
+            p_ps = next_flip()
             for j in range(SUBS):
                 nc.tensor.transpose(p_ps[:, j, :], q_raw[h][:, n * SUBS + j, :], ident[:])
             for j in range(SUBS):
                 nc.tensor.transpose(p_ps[:, SUBS + j, :], k_raw[h][:, n * SUBS + j, :], ident[:])
+            bstate[("p", b)] = p_ps
+
+        def prep_copy(b):
+            h, n = blocks[b]
+            p_ps = bstate[("p", b)]
             nc.vector.tensor_copy(out=xT[h][:, :, n * W:(n + 1) * W],
                                   in_=p_ps[:].rearrange("p (a j) c -> p a (j c)", a=2))
-            v_g = vgp.tile([P, P, 4], BF16, align_bytes=64)
+
+        def prep_v(b):
+            h, n = blocks[b]
+            v_g = vgp.tile([P, P, 4], BF16, name="v_g", align_bytes=64)
             nc.vector.tensor_copy(out=v_g[:], in_=v_raw[h][:, n * SUBS:(n + 1) * SUBS, :].rearrange("p t d -> p d t"))
+            bstate[("vg", b)] = v_g
+
+        def quant_v(b):
+            h, n = blocks[b]
+            v_g = bstate[("vg", b)]
             nc.vector.quantize_mx(out=v_words[h][:, n, :].bitcast(FP8X4), scales=v_scales[h][:, n, :],
                                   in_=v_g[:].rearrange("p d t -> p (d t)"))
 
-        state = {}
+        def edge_pe(b):
+            h, n = blocks[b]
+            se = s_edge[b % 2]
+            for j in range(SUBS):
+                row = n * SUBS + j
+                nc.tensor.matmul(se[:, j, :], lhsT=ident[:], rhs=mask[:, 1, :], start=True, stop=False)
+                nc.tensor.matmul(se[:, j, :], lhsT=xT[h][:, 0, row * P:(row + 1) * P],
+                                 rhs=xT[h][:, 1, row * P:(row + 1) * P], start=False, stop=True)
 
-        def scores(i, h, n, qt):
-            s_ps = ps_s.tile([P, 2 * W], F32)
+        def edge_max(b):
+            m_edge = stat.tile([P, SUBS], F32, name="m_edge")
+            nc.vector.tensor_reduce(out=m_edge[:], in_=s_edge[b % 2][:], axis=AX.X, op=ALU.max)
+            dn = stat.tile([P, 2, SUBS], F32, name="dn")
+            bstate[("me", b)] = m_edge
+            bstate[("dn", b)] = dn
+
+        def main_pe(i):
+            h, n, qt = tiles[i]
+            sm = s_main[i % 3]
             row = n * SUBS + qt
             qT = xT[h][:, 0, row * P:(row + 1) * P]
             k0 = (row - SUBS) * P
-            first = 0 if n > 0 else SUBS - qt
             if n > 0:
-                nc.tensor.matmul(s_ps[:, 0:P], lhsT=ident[:], rhs=mask[:, 0, :], start=True, stop=False)
-            nc.tensor.matmul(s_ps[:, W:W + P], lhsT=ident[:], rhs=mask[:, 1, :], start=True, stop=False)
-            if n > 0:
-                nc.tensor.matmul(s_ps[:, 0:P], lhsT=qT, rhs=xT[h][:, 1, k0:k0 + P], start=False, stop=True)
-            lo = 1 if n > 0 else first
-            if lo < SUBS:
-                nc.tensor.matmul(s_ps[:, lo * P:W], lhsT=qT, rhs=xT[h][:, 1, k0 + lo * P:k0 + W], start=True, stop=True)
-            nc.tensor.matmul(s_ps[:, W:W + P], lhsT=qT, rhs=xT[h][:, 1, k0 + W:k0 + W + P], start=False, stop=True)
-            mm = stat.tile([P, 2], F32)
-            nm = stat.tile([P, 1], F32)
-            nc.vector.tensor_reduce(out=mm[:, 1:2], in_=s_ps[:, W:W + P], axis=AX.X, op=ALU.max)
-            if first < SUBS:
-                nc.vector.tensor_reduce(out=mm[:, 0:1], in_=s_ps[:, first * P:W], axis=AX.X, op=ALU.max)
-                nc.vector.tensor_scalar(out=nm[:], in0=mm[:, 0:1], scalar1=mm[:, 1:2], scalar2=-SCALE,
-                                        op0=ALU.max, op1=ALU.mult)
+                nc.tensor.matmul(sm[:, 0:P], lhsT=ident[:], rhs=mask[:, 0, :], start=True, stop=False)
+                nc.tensor.matmul(sm[:, 0:P], lhsT=qT, rhs=xT[h][:, 1, k0:k0 + P], start=False, stop=True)
+                nc.tensor.matmul(sm[:, P:W], lhsT=qT, rhs=xT[h][:, 1, k0 + P:k0 + W], start=True, stop=True)
+            elif qt == 0:
+                nc.tensor.matmul(sm[:, W - P:W], lhsT=ident[:], rhs=mask[:, 2, :], start=True, stop=True)
             else:
-                nc.vector.tensor_scalar(out=nm[:], in0=mm[:, 1:2], scalar1=-SCALE, scalar2=None, op0=ALU.mult)
-            e_sb = ep.tile([P, 5 * P], BF16)
-            dn = stat.tile([P, 2], F32)
-            if first < SUBS:
-                nc.scalar.activation(out=e_sb[:, first * P:W], in_=s_ps[:, first * P:W], func=ACTF.Exp,
-                                     bias=nm[:], scale=SCALE, accum_out=dn[:, 0:1])
-            nc.scalar.activation(out=e_sb[:, W:W + P], in_=s_ps[:, W:W + P], func=ACTF.Exp,
-                                 bias=nm[:], scale=SCALE, accum_out=dn[:, 1:2])
-            state[i] = {"e": e_sb, "dn": dn, "first": first}
+                nc.tensor.matmul(sm[:, W - qt * P:W], lhsT=qT, rhs=xT[h][:, 1, 0:qt * P], start=True, stop=True)
 
-        def flip(i, h, n, qt):
-            st = state[i]
-            first = st["first"]
-            e_sb = st["e"]
-            t_ps = ps_t.tile([P, 5, P], BF16)
+        def lo_col(i):
+            h, n, qt = tiles[i]
+            if n > 0:
+                return 0
+            return W - max(qt, 1) * P
+
+        def main_max(i):
+            h, n, qt = tiles[i]
+            m_main = stat.tile([P, 1], F32, name="m_main")
+            nm = stat.tile([P, 1], F32, name="nm")
+            nc.vector.tensor_reduce(out=m_main[:], in_=s_main[i % 3][:, lo_col(i):W], axis=AX.X, op=ALU.max)
+            nc.vector.tensor_scalar(out=nm[:], in0=m_main[:], scalar1=bstate[("me", i // SUBS)][:, qt:qt + 1],
+                                    scalar2=-SCALE, op0=ALU.max, op1=ALU.mult)
+            state[("nm", i)] = nm
+
+        def exps(i):
+            h, n, qt = tiles[i]
+            b = i // SUBS
+            nm = state[("nm", i)]
+            dn = bstate[("dn", b)]
+            e_sb = ep.tile([P, 5 * P], BF16, name="e_sb")
+            lo = lo_col(i)
+            nc.scalar.activation(out=e_sb[:, lo:W], in_=s_main[i % 3][:, lo:W], func=ACTF.Exp,
+                                 bias=nm[:], scale=SCALE, accum_out=dn[:, 0, qt:qt + 1])
+            nc.scalar.activation(out=e_sb[:, W:W + P], in_=s_edge[b % 2][:, qt, :], func=ACTF.Exp,
+                                 bias=nm[:], scale=SCALE, accum_out=dn[:, 1, qt:qt + 1])
+            state[("e", i)] = e_sb
+
+        def flip_pe(i):
+            h, n, qt = tiles[i]
+            e_sb = state[("e", i)]
+            t_ps = next_flip()
+            first = 0 if n > 0 else SUBS - qt
             for w in range(first, 5):
                 nc.tensor.transpose(t_ps[:, w, :], e_sb[:, w * P:(w + 1) * P], ident[:])
+            state[("t", i)] = t_ps
+
+        def regroup(i):
+            h, n, qt = tiles[i]
+            t_ps = state[("t", i)]
             g = grouped[qt]
             ra = SUBS - qt
             if n > 0:
                 nc.scalar.copy(out=g[:, 0, :, qt:SUBS], in_=t_ps[:, 0:ra, :].rearrange("p t c -> p c t"))
             nc.scalar.copy(out=g[:, 1, :, 0:qt + 1], in_=t_ps[:, ra:5, :].rearrange("p t c -> p c t"))
 
-        def finish(i, h, n, qt):
-            st = state[i]
+        def quant(i):
+            h, n, qt = tiles[i]
             g = grouped[qt]
-            e_words = wp.tile([P, 2 * P], U32, align_bytes=64)
-            e_scales = wp.tile([P, 2 * P], U8, align_bytes=64)
+            e_words = wp.tile([P, 2 * P], U32, name="e_words", align_bytes=64)
+            e_scales = wp.tile([P, 2 * P], U8, name="e_scales", align_bytes=64)
             a0 = 0 if n > 0 else 1
             nc.vector.quantize_mx(out=e_words[:, a0 * P:].bitcast(FP8X4), scales=e_scales[:, a0 * P:],
                                   in_=g[:, a0:, :, :].rearrange("p a c t -> p (a c t)"))
-            o_ps = ps_o.tile([P, P], F32)
+            state[("w", i)] = (e_words, e_scales)
+
+        def mx(i):
+            h, n, qt = tiles[i]
+            e_words, e_scales = state[("w", i)]
+            a0 = 0 if n > 0 else 1
             for a in range(a0, 2):
-                nc.tensor.matmul_mx(out=o_ps[:], lhsT=e_words[:, a * P:(a + 1) * P].bitcast(FP8X4),
+                nc.tensor.matmul_mx(out=o_ps[:, qt, :], lhsT=e_words[:, a * P:(a + 1) * P].bitcast(FP8X4),
                                     lhsT_scale=e_scales[:, a * P:(a + 1) * P],
                                     rhs=v_words[h][:, n - 1 + a, :].bitcast(FP8X4),
                                     rhs_scale=v_scales[h][:, n - 1 + a, :],
                                     start=(a == a0), stop=(a == 1))
-            dn = st["dn"]
-            rd = stat.tile([P, 1], F32)
-            if st["first"] < SUBS:
-                ds = stat.tile([P, 1], F32)
-                nc.vector.tensor_tensor(out=ds[:], in0=dn[:, 0:1], in1=dn[:, 1:2], op=ALU.add)
-                nc.vector.reciprocal(out=rd[:], in_=ds[:])
-            else:
-                nc.vector.reciprocal(out=rd[:], in_=dn[:, 1:2])
-            if qt == 0:
-                o_sb = op.tile([P, SUBS, P], F32)
-                state["o"] = o_sb
-            o_sb = state["o"]
-            nc.vector.tensor_scalar(out=o_sb[:, qt, :], in0=o_ps[:], scalar1=rd[:], scalar2=None, op0=ALU.mult)
-            if qt == SUBS - 1:
-                r0 = h * NS + n * SUBS
-                nc.sync.dma_start(out=ov[:, r0:r0 + SUBS, :], in_=o_sb[:])
 
-        tiles = [(h, n, qt) for h in range(H) for n in range(NB) for qt in range(SUBS)]
-        blocks = [(h, n) for h in range(H) for n in range(NB)]
-        NT = len(tiles)
-        prep(*blocks[0])
-        prep(*blocks[1])
-        for s in range(NT + 2):
-            if s < NT:
-                if s % SUBS == 1 and s // SUBS + 2 < len(blocks):
-                    prep(*blocks[s // SUBS + 2])
-                scores(s, *tiles[s])
-            if 0 <= s - 1 < NT:
-                flip(s - 1, *tiles[s - 1])
-            if 0 <= s - 2 < NT:
-                finish(s - 2, *tiles[s - 2])
+        def finish(b):
+            h, n = blocks[b]
+            dn = bstate[("dn", b)]
+            ds = stat.tile([P, SUBS], F32, name="ds")
+            rd = stat.tile([P, SUBS], F32, name="rd")
+            nc.vector.tensor_tensor(out=ds[:], in0=dn[:, 0, :], in1=dn[:, 1, :], op=ALU.add)
+            nc.vector.reciprocal(out=rd[:], in_=ds[:])
+            o_sb = op.tile([P, SUBS, P], F32, name="o_sb")
+            nc.vector.tensor_tensor(out=o_sb[:], in0=o_ps[:], in1=rd[:].unsqueeze(2).to_broadcast([P, SUBS, P]),
+                                    op=ALU.mult)
+            r0 = h * NS + n * SUBS
+            nc.sync.dma_start(out=ov[:, r0:r0 + SUBS, :], in_=o_sb[:])
+
+        for b in range(2):
+            prep_pe(b)
+            prep_copy(b)
+            prep_v(b)
+        quant_v(0)
+        quant_v(1)
+        edge_pe(0)
+        edge_max(0)
+
+        def ok(i):
+            return 0 <= i < NT
+
+        for s in range(NT + L_OUT + SUBS):
+            ph = s % SUBS
+            i_out = s - L_OUT
+            if i_out >= SUBS - 1 and i_out % SUBS == SUBS - 1 and i_out < NT:
+                finish(i_out // SUBS)
+            if s % (NB * SUBS) in (4, 12) and s // (NB * SUBS) + 1 < H:
+                half = 0 if s % (NB * SUBS) == 4 else NS // 2
+                load(s // (NB * SUBS) + 1, half, half + NS // 2)
+            if ok(s - L_FLIP):
+                flip_pe(s - L_FLIP)
+            b_prep = s // SUBS + 2
+            if ph == 2 and b_prep < NBLK:
+                prep_pe(b_prep)
+            if ok(s):
+                main_pe(s)
+            b_edge = s // SUBS + 1
+            if ph == 3 and b_edge < NBLK:
+                edge_pe(b_edge)
+            if ok(s - L_MX):
+                mx(s - L_MX)
+            if ok(s - L_MAX):
+                main_max(s - L_MAX)
+            if ok(s - L_EXP):
+                exps(s - L_EXP)
+            if ok(s - L_FLIP):
+                regroup(s - L_FLIP)
+            if ok(s - L_QUANT):
+                quant(s - L_QUANT)
+            if ph == 0 and 0 < s // SUBS < NBLK:
+                edge_max(s // SUBS)
+            if ph == 2 and b_prep < NBLK:
+                prep_copy(b_prep)
+            if ph == 3 and b_prep < NBLK:
+                prep_v(b_prep)
+            if ph == 0 and 1 < s // SUBS + 1 < NBLK:
+                quant_v(s // SUBS + 1)

@@ -26,9 +26,10 @@ FLOPS = 2 * (2 * NB - 1) * H * 2 * W * W * P
 L_MAX = 1
 L_EXP = 2
 L_FLIP = 3
-L_QUANT = 4
-L_MX = 5
-L_OUT = 6
+L_QUANT = 5
+L_MX = 6
+L_OUT = 7
+VIA_GPSIMD = (1, 3)
 
 
 def tile_baseattention_t_kernel(tc, q, k, v, out):
@@ -44,6 +45,7 @@ def tile_baseattention_t_kernel(tc, q, k, v, out):
         ep = ctx.enter_context(tc.tile_pool(name="ep", bufs=3))
         wp = ctx.enter_context(tc.tile_pool(name="wp", bufs=3))
         vgp = ctx.enter_context(tc.tile_pool(name="vgp", bufs=2))
+        tsp = ctx.enter_context(tc.tile_pool(name="tsp", bufs=3))
         op = ctx.enter_context(tc.tile_pool(name="op", bufs=3))
         psum = ctx.enter_context(tc.psum_pool(name="psum", bufs=1))
         ctx.enter_context(tc.manual_schedule())
@@ -209,9 +211,19 @@ def tile_baseattention_t_kernel(tc, q, k, v, out):
             t_ps = state[("t", i)]
             g = grouped[qt]
             ra = SUBS - qt
-            if n > 0:
-                nc.scalar.copy(out=g[:, 0, :, qt:SUBS], in_=t_ps[:, 0:ra, :].rearrange("p t c -> p c t"))
-            nc.scalar.copy(out=g[:, 1, :, 0:qt + 1], in_=t_ps[:, ra:5, :].rearrange("p t c -> p c t"))
+            if qt in VIA_GPSIMD:
+                first = 0 if n > 0 else ra
+                t_sb = tsp.tile([P, 5, P], BF16, name="t_sb")
+                nc.scalar.copy(out=t_sb[:, first:5, :], in_=t_ps[:, first:5, :])
+                if n > 0:
+                    nc.gpsimd.tensor_scalar(out=g[:, 0, :, qt:SUBS], in0=t_sb[:, 0:ra, :].rearrange("p t c -> p c t"),
+                                            scalar1=1.0, scalar2=0.0, op0=ALU.mult, op1=ALU.add)
+                nc.gpsimd.tensor_scalar(out=g[:, 1, :, 0:qt + 1], in0=t_sb[:, ra:5, :].rearrange("p t c -> p c t"),
+                                        scalar1=1.0, scalar2=0.0, op0=ALU.mult, op1=ALU.add)
+            else:
+                if n > 0:
+                    nc.scalar.copy(out=g[:, 0, :, qt:SUBS], in_=t_ps[:, 0:ra, :].rearrange("p t c -> p c t"))
+                nc.scalar.copy(out=g[:, 1, :, 0:qt + 1], in_=t_ps[:, ra:5, :].rearrange("p t c -> p c t"))
 
         def quant(i):
             h, n, qt = tiles[i]

@@ -178,8 +178,13 @@ def tile_baseattention_t_kernel(tc, q, k, v, out):
         def main_max(i):
             h, n, qt = tiles[i]
             m_main = stat.tile([P, 1], F32, name="m_main")
-            nm = stat.tile([P, 1], F32, name="nm")
             nc.vector.tensor_reduce(out=m_main[:], in_=s_main[i % 3][:, lo_col(i):W], axis=AX.X, op=ALU.max)
+            state[("mm", i)] = m_main
+
+        def combine(i):
+            h, n, qt = tiles[i]
+            m_main = state[("mm", i)]
+            nm = stat.tile([P, 1], F32, name="nm")
             nc.vector.tensor_scalar(out=nm[:], in0=m_main[:], scalar1=bstate[("me", i // SUBS)][:, qt:qt + 1],
                                     scalar2=-SCALE, op0=ALU.max, op1=ALU.mult)
             state[("nm", i)] = nm
@@ -246,13 +251,20 @@ def tile_baseattention_t_kernel(tc, q, k, v, out):
                                     rhs_scale=v_scales[h][:, n - 1 + a, :],
                                     start=(a == a0), stop=(a == 1))
 
-        def finish(b):
-            h, n = blocks[b]
+        def den_add(b):
             dn = bstate[("dn", b)]
             ds = stat.tile([P, SUBS], F32, name="ds")
-            rd = stat.tile([P, SUBS], F32, name="rd")
             nc.vector.tensor_tensor(out=ds[:], in0=dn[:, 0, :], in1=dn[:, 1, :], op=ALU.add)
-            nc.vector.reciprocal(out=rd[:], in_=ds[:])
+            bstate[("ds", b)] = ds
+
+        def den_recip(b):
+            rd = stat.tile([P, SUBS], F32, name="rd")
+            nc.vector.reciprocal(out=rd[:], in_=bstate[("ds", b)][:])
+            bstate[("rd", b)] = rd
+
+        def finish(b):
+            h, n = blocks[b]
+            rd = bstate[("rd", b)]
             o_sb = op.tile([P, SUBS, P], F32, name="o_sb")
             nc.vector.tensor_tensor(out=o_sb[:], in0=o_ps[:], in1=rd[:].unsqueeze(2).to_broadcast([P, SUBS, P]),
                                     op=ALU.mult)
@@ -293,12 +305,18 @@ def tile_baseattention_t_kernel(tc, q, k, v, out):
                 mx(s - L_MX)
             if ok(s - L_MAX):
                 main_max(s - L_MAX)
+            if ok(s - L_QUANT):
+                quant(s - L_QUANT)
+            if ok(s - L_MAX):
+                combine(s - L_MAX)
             if ok(s - L_EXP):
                 exps(s - L_EXP)
             if ok(s - L_FLIP):
                 regroup(s - L_FLIP)
-            if ok(s - L_QUANT):
-                quant(s - L_QUANT)
+            i_den = s - L_EXP - 1
+            den_due = i_den >= 0 and i_den % SUBS == SUBS - 1 and i_den < NT
+            if den_due:
+                den_add(i_den // SUBS)
             if ph == 0 and 0 < s // SUBS < NBLK:
                 edge_max(s // SUBS)
             if ph == 2 and b_prep < NBLK:
@@ -307,3 +325,5 @@ def tile_baseattention_t_kernel(tc, q, k, v, out):
                 prep_v(b_prep)
             if ph == 0 and 1 < s // SUBS + 1 < NBLK:
                 quant_v(s // SUBS + 1)
+            if den_due:
+                den_recip(i_den // SUBS)

@@ -29,7 +29,7 @@ L_FLIP = 3
 L_QUANT = 5
 L_MX = 6
 L_OUT = 7
-VIA_GPSIMD = (1, 3)
+SMALL = 2
 
 
 def tile_baseattention_t_kernel(tc, q, k, v, out):
@@ -129,7 +129,8 @@ def tile_baseattention_t_kernel(tc, q, k, v, out):
         def prep_v(b):
             h, n = blocks[b]
             v_g = vgp.tile([P, P, 4], BF16, name="v_g", align_bytes=64)
-            nc.vector.tensor_copy(out=v_g[:], in_=v_raw[h][:, n * SUBS:(n + 1) * SUBS, :].rearrange("p t d -> p d t"))
+            nc.gpsimd.tensor_scalar(out=v_g[:], in0=v_raw[h][:, n * SUBS:(n + 1) * SUBS, :].rearrange("p t d -> p d t"),
+                                    scalar1=1.0, scalar2=0.0, op0=ALU.mult, op1=ALU.add)
             bstate[("vg", b)] = v_g
 
         def quant_v(b):
@@ -216,19 +217,17 @@ def tile_baseattention_t_kernel(tc, q, k, v, out):
             t_ps = state[("t", i)]
             g = grouped[qt]
             ra = SUBS - qt
-            if qt in VIA_GPSIMD:
-                first = 0 if n > 0 else ra
-                t_sb = tsp.tile([P, 5, P], BF16, name="t_sb")
-                nc.scalar.copy(out=t_sb[:, first:5, :], in_=t_ps[:, first:5, :])
-                if n > 0:
-                    nc.gpsimd.tensor_scalar(out=g[:, 0, :, qt:SUBS], in0=t_sb[:, 0:ra, :].rearrange("p t c -> p c t"),
+            passes = [(qt + 1, 1, ra, 0)]
+            if n > 0:
+                passes.append((ra, 0, 0, qt))
+            for r, a, w0, t0 in sorted(passes):
+                if r <= SMALL:
+                    t_sb = tsp.tile([P, SMALL, P], BF16, name="t_sb")
+                    nc.scalar.copy(out=t_sb[:, 0:r, :], in_=t_ps[:, w0:w0 + r, :])
+                    nc.gpsimd.tensor_scalar(out=g[:, a, :, t0:t0 + r], in0=t_sb[:, 0:r, :].rearrange("p t c -> p c t"),
                                             scalar1=1.0, scalar2=0.0, op0=ALU.mult, op1=ALU.add)
-                nc.gpsimd.tensor_scalar(out=g[:, 1, :, 0:qt + 1], in0=t_sb[:, ra:5, :].rearrange("p t c -> p c t"),
-                                        scalar1=1.0, scalar2=0.0, op0=ALU.mult, op1=ALU.add)
-            else:
-                if n > 0:
-                    nc.scalar.copy(out=g[:, 0, :, qt:SUBS], in_=t_ps[:, 0:ra, :].rearrange("p t c -> p c t"))
-                nc.scalar.copy(out=g[:, 1, :, 0:qt + 1], in_=t_ps[:, ra:5, :].rearrange("p t c -> p c t"))
+                else:
+                    nc.scalar.copy(out=g[:, a, :, t0:t0 + r], in_=t_ps[:, w0:w0 + r, :].rearrange("p t c -> p c t"))
 
         def quant(i):
             h, n, qt = tiles[i]
@@ -323,7 +322,7 @@ def tile_baseattention_t_kernel(tc, q, k, v, out):
                 prep_copy(b_prep)
             if ph == 3 and b_prep < NBLK:
                 prep_v(b_prep)
-            if ph == 0 and 1 < s // SUBS + 1 < NBLK:
+            if ph == 1 and 1 < s // SUBS + 1 < NBLK:
                 quant_v(s // SUBS + 1)
             if den_due:
                 den_recip(i_den // SUBS)

@@ -155,7 +155,7 @@ def tile_baseattention_t_kernel(tc, q, k, v, out):
             bstate[("me", b)] = m_edge
             bstate[("dn", b)] = dn
 
-        def main_pe(i):
+        def main_pe_first(i):
             h, n, qt = tiles[i]
             sm = s_main[i % 3]
             row = n * SUBS + qt
@@ -164,6 +164,14 @@ def tile_baseattention_t_kernel(tc, q, k, v, out):
             if n > 0:
                 nc.tensor.matmul(sm[:, 0:P], lhsT=ident[:], rhs=mask[:, 0, :], start=True, stop=False)
                 nc.tensor.matmul(sm[:, 0:P], lhsT=qT, rhs=xT[h][:, 1, k0:k0 + P], start=False, stop=True)
+
+        def main_pe_rest(i):
+            h, n, qt = tiles[i]
+            sm = s_main[i % 3]
+            row = n * SUBS + qt
+            qT = xT[h][:, 0, row * P:(row + 1) * P]
+            k0 = (row - SUBS) * P
+            if n > 0:
                 nc.tensor.matmul(sm[:, P:W], lhsT=qT, rhs=xT[h][:, 1, k0 + P:k0 + W], start=True, stop=True)
             elif qt == 0:
                 nc.tensor.matmul(sm[:, W - P:W], lhsT=ident[:], rhs=mask[:, 2, :], start=True, stop=True)
@@ -296,12 +304,14 @@ def tile_baseattention_t_kernel(tc, q, k, v, out):
             if ph == 2 and b_prep < NBLK:
                 prep_pe(b_prep)
             if ok(s):
-                main_pe(s)
+                main_pe_first(s)
+            if ok(s - L_MX):
+                mx(s - L_MX)
+            if ok(s):
+                main_pe_rest(s)
             b_edge = s // SUBS + 1
             if ph == 3 and b_edge < NBLK:
                 edge_pe(b_edge)
-            if ok(s - L_MX):
-                mx(s - L_MX)
             if ok(s - L_MAX):
                 main_max(s - L_MAX)
             if ok(s - L_QUANT):

@@ -63,7 +63,8 @@ def tile_baseattention_t_kernel(tc, q, k, v, out):
             nc.sync.dma_start(out=k_raw[h][:, a:b, :], in_=kv[:, h * NS + a:h * NS + b, :])
             nc.sync.dma_start(out=v_raw[h][:, a:b, :], in_=vv[:, h * NS + a:h * NS + b, :])
 
-        load(0, 0, 8)
+        load(0, 0, 4)
+        load(0, 4, 8)
         load(0, 8, 16)
         load(0, 16, NS)
 
@@ -261,7 +262,7 @@ def tile_baseattention_t_kernel(tc, q, k, v, out):
         def den_add(b):
             dn = bstate[("dn", b)]
             ds = stat.tile([P, SUBS], F32, name="ds")
-            nc.vector.tensor_tensor(out=ds[:], in0=dn[:, 0, :], in1=dn[:, 1, :], op=ALU.add)
+            nc.gpsimd.tensor_tensor(out=ds[:], in0=dn[:, 0, :], in1=dn[:, 1, :], op=ALU.add)
             bstate[("ds", b)] = ds
 
         def den_recip(b):
@@ -278,14 +279,12 @@ def tile_baseattention_t_kernel(tc, q, k, v, out):
             r0 = h * NS + n * SUBS
             nc.sync.dma_start(out=ov[:, r0:r0 + SUBS, :], in_=o_sb[:])
 
-        for b in range(2):
-            prep_pe(b)
-            prep_copy(b)
-            prep_v(b)
-        quant_v(0)
-        quant_v(1)
+        prep_pe(0)
+        prep_copy(0)
         edge_pe(0)
         edge_max(0)
+        prep_v(0)
+        prep_v(1)
 
         def ok(i):
             return 0 <= i < NT
@@ -309,6 +308,8 @@ def tile_baseattention_t_kernel(tc, q, k, v, out):
                 mx(s - L_MX)
             if ok(s):
                 main_pe_rest(s)
+            if s == 0:
+                prep_pe(1)
             b_edge = s // SUBS + 1
             if ph == 3 and b_edge < NBLK:
                 edge_pe(b_edge)
@@ -328,11 +329,15 @@ def tile_baseattention_t_kernel(tc, q, k, v, out):
                 den_add(i_den // SUBS)
             if ph == 0 and 0 < s // SUBS < NBLK:
                 edge_max(s // SUBS)
+            if s == 0:
+                prep_copy(1)
+            if s in (1, 2):
+                quant_v(s - 1)
             if ph == 2 and b_prep < NBLK:
                 prep_copy(b_prep)
             if ph == 3 and b_prep < NBLK:
                 prep_v(b_prep)
             if ph == 1 and 1 < s // SUBS + 1 < NBLK:
                 quant_v(s // SUBS + 1)
-            if den_due:
-                den_recip(i_den // SUBS)
+            if i_den - 1 >= 0 and (i_den - 1) % SUBS == SUBS - 1 and i_den - 1 < NT:
+                den_recip((i_den - 1) // SUBS)

@@ -63,8 +63,7 @@ def tile_baseattention_t_kernel(tc, q, k, v, out):
             nc.sync.dma_start(out=k_raw[h][:, a:b, :], in_=kv[:, h * NS + a:h * NS + b, :])
             nc.sync.dma_start(out=v_raw[h][:, a:b, :], in_=vv[:, h * NS + a:h * NS + b, :])
 
-        load(0, 0, 4)
-        load(0, 4, 8)
+        load(0, 0, 8)
         load(0, 8, 16)
         load(0, 16, NS)
 
@@ -98,6 +97,7 @@ def tile_baseattention_t_kernel(tc, q, k, v, out):
         s_edge = [psum.tile([P, SUBS, P], F32, name="s_edge%d" % j) for j in range(2)]
         flipped = [psum.tile([P, 2 * SUBS, P], BF16, name="flipped%d" % j) for j in range(2)]
         o_ps = psum.tile([P, SUBS, P], F32, name="o_ps")
+        edge_bf = [t[:].rearrange("p j c -> p (j c)").bitcast(BF16).rearrange("p (j c) -> p j c", c=P) for t in s_edge]
 
         tiles = [(h, n, qt) for h in range(H) for n in range(NB) for qt in range(SUBS)]
         blocks = [(h, n) for h in range(H) for n in range(NB)]
@@ -112,9 +112,8 @@ def tile_baseattention_t_kernel(tc, q, k, v, out):
             ring["flip"] = 1 - j
             return flipped[j]
 
-        def prep_pe(b):
+        def prep_pe(b, p_ps):
             h, n = blocks[b]
-            p_ps = next_flip()
             for j in range(SUBS):
                 nc.tensor.transpose(p_ps[:, j, :], q_raw[h][:, n * SUBS + j, :], ident[:])
             for j in range(SUBS):
@@ -125,7 +124,7 @@ def tile_baseattention_t_kernel(tc, q, k, v, out):
             h, n = blocks[b]
             p_ps = bstate[("p", b)]
             nc.vector.tensor_copy(out=xT[h][:, :, n * W:(n + 1) * W],
-                                  in_=p_ps[:].rearrange("p (a j) c -> p a (j c)", a=2))
+                                  in_=p_ps.rearrange("p (a j) c -> p a (j c)", a=2))
 
         def prep_v(b):
             h, n = blocks[b]
@@ -262,7 +261,7 @@ def tile_baseattention_t_kernel(tc, q, k, v, out):
         def den_add(b):
             dn = bstate[("dn", b)]
             ds = stat.tile([P, SUBS], F32, name="ds")
-            nc.gpsimd.tensor_tensor(out=ds[:], in0=dn[:, 0, :], in1=dn[:, 1, :], op=ALU.add)
+            nc.vector.tensor_tensor(out=ds[:], in0=dn[:, 0, :], in1=dn[:, 1, :], op=ALU.add)
             bstate[("ds", b)] = ds
 
         def den_recip(b):
@@ -279,12 +278,14 @@ def tile_baseattention_t_kernel(tc, q, k, v, out):
             r0 = h * NS + n * SUBS
             nc.sync.dma_start(out=ov[:, r0:r0 + SUBS, :], in_=o_sb[:])
 
-        prep_pe(0)
-        prep_copy(0)
+        for b in range(2):
+            prep_pe(b, flipped[b][:])
+            prep_copy(b)
+            prep_v(b)
+        quant_v(0)
+        quant_v(1)
         edge_pe(0)
         edge_max(0)
-        prep_v(0)
-        prep_v(1)
 
         def ok(i):
             return 0 <= i < NT
@@ -301,15 +302,13 @@ def tile_baseattention_t_kernel(tc, q, k, v, out):
                 flip_pe(s - L_FLIP)
             b_prep = s // SUBS + 2
             if ph == 2 and b_prep < NBLK:
-                prep_pe(b_prep)
+                prep_pe(b_prep, edge_bf[(s // SUBS + 1) % 2])
             if ok(s):
                 main_pe_first(s)
             if ok(s - L_MX):
                 mx(s - L_MX)
             if ok(s):
                 main_pe_rest(s)
-            if s == 0:
-                prep_pe(1)
             b_edge = s // SUBS + 1
             if ph == 3 and b_edge < NBLK:
                 edge_pe(b_edge)
@@ -329,15 +328,11 @@ def tile_baseattention_t_kernel(tc, q, k, v, out):
                 den_add(i_den // SUBS)
             if ph == 0 and 0 < s // SUBS < NBLK:
                 edge_max(s // SUBS)
-            if s == 0:
-                prep_copy(1)
-            if s in (1, 2):
-                quant_v(s - 1)
             if ph == 2 and b_prep < NBLK:
                 prep_copy(b_prep)
             if ph == 3 and b_prep < NBLK:
                 prep_v(b_prep)
             if ph == 1 and 1 < s // SUBS + 1 < NBLK:
                 quant_v(s // SUBS + 1)
-            if i_den - 1 >= 0 and (i_den - 1) % SUBS == SUBS - 1 and i_den - 1 < NT:
-                den_recip((i_den - 1) // SUBS)
+            if den_due:
+                den_recip(i_den // SUBS)

from contextlib import ExitStack

import concourse.mybir as mybir
from concourse.masks import make_identity

F32 = mybir.dt.float32
BF16 = mybir.dt.bfloat16
U32 = mybir.dt.uint32
U8 = mybir.dt.uint8
FP8X4 = mybir.dt.float8_e4m3fn_x4
ALU = mybir.AluOpType
ACTF = mybir.ActivationFunctionType
AX = mybir.AxisListType

P = 128
H = 4
T = 4096
W = 512
NB = T // W
SUBS = W // P
NS = T // P
SCALE = 128.0 ** -0.5
NEG = -(2.0 ** 80)
FLOPS = 2 * (2 * NB - 1) * H * 2 * W * W * P

L_MAX = 1
L_EXP = 2
L_FLIP = 3
L_QUANT = 5
L_MX = 6
L_OUT = 7
SMALL = 2


def tile_baseattention_t_kernel(tc, q, k, v, out):
    nc = tc.nc
    qv = q.rearrange("b h (s p) d -> p (b h s) d", p=P)
    kv = k.rearrange("b h (s p) d -> p (b h s) d", p=P)
    vv = v.rearrange("b h (s p) d -> p (b h s) d", p=P)
    ov = out.rearrange("b h (s p) d -> p (b h s) d", p=P)

    with ExitStack() as ctx:
        const = ctx.enter_context(tc.tile_pool(name="const", bufs=1))
        stat = ctx.enter_context(tc.tile_pool(name="stat", bufs=4))
        ep = ctx.enter_context(tc.tile_pool(name="ep", bufs=3))
        wp = ctx.enter_context(tc.tile_pool(name="wp", bufs=3))
        vgp = ctx.enter_context(tc.tile_pool(name="vgp", bufs=2))
        tsp = ctx.enter_context(tc.tile_pool(name="tsp", bufs=3))
        op = ctx.enter_context(tc.tile_pool(name="op", bufs=3))
        psum = ctx.enter_context(tc.psum_pool(name="psum", bufs=1))
        ctx.enter_context(tc.manual_schedule())

        q_raw = []
        k_raw = []
        v_raw = []
        for h in range(H):
            q_raw.append(const.tile([P, NS, P], BF16, name="q_raw%d" % h))
            k_raw.append(const.tile([P, NS, P], BF16, name="k_raw%d" % h))
            v_raw.append(const.tile([P, NS, P], BF16, name="v_raw%d" % h))

        def load(h, a, b):
            nc.sync.dma_start(out=q_raw[h][:, a:b, :], in_=qv[:, h * NS + a:h * NS + b, :])
            nc.sync.dma_start(out=k_raw[h][:, a:b, :], in_=kv[:, h * NS + a:h * NS + b, :])
            nc.sync.dma_start(out=v_raw[h][:, a:b, :], in_=vv[:, h * NS + a:h * NS + b, :])

        load(0, 0, 8)
        load(0, 8, 16)
        load(0, 16, NS)

        ident = const.tile([P, P], BF16, name="ident")
        make_identity(nc, ident[:])
        mask_f = const.tile([P, 3, P], F32, name="mask_f")
        nc.gpsimd.memset(mask_f[:, 0:2, :], 0.0)
        nc.gpsimd.memset(mask_f[:, 2, :], NEG)
        nc.gpsimd.affine_select(out=mask_f[:, 0, :], in_=mask_f[:, 0, :], compare_op=ALU.is_ge, fill=NEG,
                                base=-1, pattern=[[1, P]], channel_multiplier=-1)
        nc.gpsimd.affine_select(out=mask_f[:, 1, :], in_=mask_f[:, 1, :], compare_op=ALU.is_ge, fill=NEG,
                                base=0, pattern=[[-1, P]], channel_multiplier=1)
        mask = const.tile([P, 3, P], BF16, name="mask")
        nc.vector.tensor_copy(out=mask[:], in_=mask_f[:])

        grouped = []
        for j in range(SUBS):
            g = const.tile([P, 2, P, 4], BF16, name="grouped%d" % j, align_bytes=64)
            nc.vector.memset(g[:].rearrange("p a c t -> p (a c t)"), 0.0)
            grouped.append(g)

        xT = []
        v_words = []
        v_scales = []
        for h in range(H):
            xT.append(const.tile([P, 2, T], BF16, name="xT%d" % h))
            v_words.append(const.tile([P, NB, P], U32, name="v_words%d" % h, align_bytes=64))
            v_scales.append(const.tile([P, NB, P], U8, name="v_scales%d" % h, align_bytes=64))

        s_main = [psum.tile([P, W], F32, name="s_main%d" % j) for j in range(3)]
        s_edge = [psum.tile([P, SUBS, P], F32, name="s_edge%d" % j) for j in range(2)]
        flipped = [psum.tile([P, 2 * SUBS, P], BF16, name="flipped%d" % j) for j in range(2)]
        o_ps = psum.tile([P, SUBS, P], F32, name="o_ps")
        edge_bf = [t[:].rearrange("p j c -> p (j c)").bitcast(BF16).rearrange("p (j c) -> p j c", c=P) for t in s_edge]

        tiles = [(h, n, qt) for h in range(H) for n in range(NB) for qt in range(SUBS)]
        blocks = [(h, n) for h in range(H) for n in range(NB)]
        NT = len(tiles)
        NBLK = len(blocks)
        state = {}
        bstate = {}
        ring = {"flip": 0}

        def next_flip():
            j = ring["flip"]
            ring["flip"] = 1 - j
            return flipped[j]

        def prep_pe(b, p_ps):
            h, n = blocks[b]
            for j in range(SUBS):
                nc.tensor.transpose(p_ps[:, j, :], q_raw[h][:, n * SUBS + j, :], ident[:])
            for j in range(SUBS):
                nc.tensor.transpose(p_ps[:, SUBS + j, :], k_raw[h][:, n * SUBS + j, :], ident[:])
            bstate[("p", b)] = p_ps

        def prep_copy(b):
            h, n = blocks[b]
            p_ps = bstate[("p", b)]
            nc.vector.tensor_copy(out=xT[h][:, :, n * W:(n + 1) * W],
                                  in_=p_ps.rearrange("p (a j) c -> p a (j c)", a=2))

        def prep_v(b):
            h, n = blocks[b]
            v_g = vgp.tile([P, P, 4], BF16, name="v_g", align_bytes=64)
            nc.gpsimd.tensor_scalar(out=v_g[:], in0=v_raw[h][:, n * SUBS:(n + 1) * SUBS, :].rearrange("p t d -> p d t"),
                                    scalar1=1.0, scalar2=0.0, op0=ALU.mult, op1=ALU.add)
            bstate[("vg", b)] = v_g

        def quant_v(b):
            h, n = blocks[b]
            v_g = bstate[("vg", b)]
            nc.vector.quantize_mx(out=v_words[h][:, n, :].bitcast(FP8X4), scales=v_scales[h][:, n, :],
                                  in_=v_g[:].rearrange("p d t -> p (d t)"))

        def edge_pe(b):
            h, n = blocks[b]
            se = s_edge[b % 2]
            for j in range(SUBS):
                row = n * SUBS + j
                nc.tensor.matmul(se[:, j, :], lhsT=ident[:], rhs=mask[:, 1, :], start=True, stop=False)
                nc.tensor.matmul(se[:, j, :], lhsT=xT[h][:, 0, row * P:(row + 1) * P],
                                 rhs=xT[h][:, 1, row * P:(row + 1) * P], start=False, stop=True)

        def edge_max(b):
            m_edge = stat.tile([P, SUBS], F32, name="m_edge")
            nc.vector.tensor_reduce(out=m_edge[:], in_=s_edge[b % 2][:], axis=AX.X, op=ALU.max)
            dn = stat.tile([P, 2, SUBS], F32, name="dn")
            bstate[("me", b)] = m_edge
            bstate[("dn", b)] = dn

        def main_pe_first(i):
            h, n, qt = tiles[i]
            sm = s_main[i % 3]
            row = n * SUBS + qt
            qT = xT[h][:, 0, row * P:(row + 1) * P]
            k0 = (row - SUBS) * P
            if n > 0:
                nc.tensor.matmul(sm[:, 0:P], lhsT=ident[:], rhs=mask[:, 0, :], start=True, stop=False)
                nc.tensor.matmul(sm[:, 0:P], lhsT=qT, rhs=xT[h][:, 1, k0:k0 + P], start=False, stop=True)

        def main_pe_rest(i):
            h, n, qt = tiles[i]
            sm = s_main[i % 3]
            row = n * SUBS + qt
            qT = xT[h][:, 0, row * P:(row + 1) * P]
            k0 = (row - SUBS) * P
            if n > 0:
                nc.tensor.matmul(sm[:, P:W], lhsT=qT, rhs=xT[h][:, 1, k0 + P:k0 + W], start=True, stop=True)
            elif qt == 0:
                nc.tensor.matmul(sm[:, W - P:W], lhsT=ident[:], rhs=mask[:, 2, :], start=True, stop=True)
            else:
                nc.tensor.matmul(sm[:, W - qt * P:W], lhsT=qT, rhs=xT[h][:, 1, 0:qt * P], start=True, stop=True)

        def lo_col(i):
            h, n, qt = tiles[i]
            if n > 0:
                return 0
            return W - max(qt, 1) * P

        def main_max(i):
            h, n, qt = tiles[i]
            m_main = stat.tile([P, 1], F32, name="m_main")
            nc.vector.tensor_reduce(out=m_main[:], in_=s_main[i % 3][:, lo_col(i):W], axis=AX.X, op=ALU.max)
            state[("mm", i)] = m_main

        def combine(i):
            h, n, qt = tiles[i]
            m_main = state[("mm", i)]
            nm = stat.tile([P, 1], F32, name="nm")
            nc.vector.tensor_scalar(out=nm[:], in0=m_main[:], scalar1=bstate[("me", i // SUBS)][:, qt:qt + 1],
                                    scalar2=-SCALE, op0=ALU.max, op1=ALU.mult)
            state[("nm", i)] = nm

        def exps(i):
            h, n, qt = tiles[i]
            b = i // SUBS
            nm = state[("nm", i)]
            dn = bstate[("dn", b)]
            e_sb = ep.tile([P, 5 * P], BF16, name="e_sb")
            lo = lo_col(i)
            nc.scalar.activation(out=e_sb[:, lo:W], in_=s_main[i % 3][:, lo:W], func=ACTF.Exp,
                                 bias=nm[:], scale=SCALE, accum_out=dn[:, 0, qt:qt + 1])
            nc.scalar.activation(out=e_sb[:, W:W + P], in_=s_edge[b % 2][:, qt, :], func=ACTF.Exp,
                                 bias=nm[:], scale=SCALE, accum_out=dn[:, 1, qt:qt + 1])
            state[("e", i)] = e_sb

        def flip_pe(i):
            h, n, qt = tiles[i]
            e_sb = state[("e", i)]
            t_ps = next_flip()
            first = 0 if n > 0 else SUBS - qt
            for w in range(first, 5):
                nc.tensor.transpose(t_ps[:, w, :], e_sb[:, w * P:(w + 1) * P], ident[:])
            state[("t", i)] = t_ps

        def regroup(i):
            h, n, qt = tiles[i]
            t_ps = state[("t", i)]
            g = grouped[qt]
            ra = SUBS - qt
            passes = [(qt + 1, 1, ra, 0)]
            if n > 0:
                passes.append((ra, 0, 0, qt))
            for r, a, w0, t0 in sorted(passes):
                if r <= SMALL:
                    t_sb = tsp.tile([P, SMALL, P], BF16, name="t_sb")
                    nc.scalar.copy(out=t_sb[:, 0:r, :], in_=t_ps[:, w0:w0 + r, :])
                    nc.gpsimd.tensor_scalar(out=g[:, a, :, t0:t0 + r], in0=t_sb[:, 0:r, :].rearrange("p t c -> p c t"),
                                            scalar1=1.0, scalar2=0.0, op0=ALU.mult, op1=ALU.add)
                else:
                    nc.scalar.copy(out=g[:, a, :, t0:t0 + r], in_=t_ps[:, w0:w0 + r, :].rearrange("p t c -> p c t"))

        def quant(i):
            h, n, qt = tiles[i]
            g = grouped[qt]
            e_words = wp.tile([P, 2 * P], U32, name="e_words", align_bytes=64)
            e_scales = wp.tile([P, 2 * P], U8, name="e_scales", align_bytes=64)
            a0 = 0 if n > 0 else 1
            nc.vector.quantize_mx(out=e_words[:, a0 * P:].bitcast(FP8X4), scales=e_scales[:, a0 * P:],
                                  in_=g[:, a0:, :, :].rearrange("p a c t -> p (a c t)"))
            state[("w", i)] = (e_words, e_scales)

        def mx(i):
            h, n, qt = tiles[i]
            e_words, e_scales = state[("w", i)]
            a0 = 0 if n > 0 else 1
            for a in range(a0, 2):
                nc.tensor.matmul_mx(out=o_ps[:, qt, :], lhsT=e_words[:, a * P:(a + 1) * P].bitcast(FP8X4),
                                    lhsT_scale=e_scales[:, a * P:(a + 1) * P],
                                    rhs=v_words[h][:, n - 1 + a, :].bitcast(FP8X4),
                                    rhs_scale=v_scales[h][:, n - 1 + a, :],
                                    start=(a == a0), stop=(a == 1))

        def den_add(b):
            dn = bstate[("dn", b)]
            ds = stat.tile([P, SUBS], F32, name="ds")
            nc.vector.tensor_tensor(out=ds[:], in0=dn[:, 0, :], in1=dn[:, 1, :], op=ALU.add)
            bstate[("ds", b)] = ds

        def den_recip(b):
            rd = stat.tile([P, SUBS], F32, name="rd")
            nc.vector.reciprocal(out=rd[:], in_=bstate[("ds", b)][:])
            bstate[("rd", b)] = rd

        def finish(b):
            h, n = blocks[b]
            rd = bstate[("rd", b)]
            o_sb = op.tile([P, SUBS, P], F32, name="o_sb")
            nc.vector.tensor_tensor(out=o_sb[:], in0=o_ps[:], in1=rd[:].unsqueeze(2).to_broadcast([P, SUBS, P]),
                                    op=ALU.mult)
            r0 = h * NS + n * SUBS
            nc.sync.dma_start(out=ov[:, r0:r0 + SUBS, :], in_=o_sb[:])

        for b in range(2):
            prep_pe(b, flipped[b][:])
            prep_copy(b)
            prep_v(b)
        quant_v(0)
        quant_v(1)
        edge_pe(0)
        edge_max(0)

        def ok(i):
            return 0 <= i < NT

        for s in range(NT + L_OUT + SUBS):
            ph = s % SUBS
            i_out = s - L_OUT
            if i_out >= SUBS - 1 and i_out % SUBS == SUBS - 1 and i_out < NT:
                finish(i_out // SUBS)
            if s % (NB * SUBS) in (4, 12) and s // (NB * SUBS) + 1 < H:
                half = 0 if s % (NB * SUBS) == 4 else NS // 2
                load(s // (NB * SUBS) + 1, half, half + NS // 2)
            if ok(s - L_FLIP):
                flip_pe(s - L_FLIP)
            b_prep = s // SUBS + 2
            if ph == 2 and b_prep < NBLK:
                prep_pe(b_prep, edge_bf[(s // SUBS + 1) % 2])
            if ok(s):
                main_pe_first(s)
            if ok(s - L_MX):
                mx(s - L_MX)
            if ok(s):
                main_pe_rest(s)
            b_edge = s // SUBS + 1
            if ph == 3 and b_edge < NBLK:
                edge_pe(b_edge)
            if ok(s - L_MAX):
                main_max(s - L_MAX)
            if ok(s - L_QUANT):
                quant(s - L_QUANT)
            if ok(s - L_MAX):
                combine(s - L_MAX)
            if ok(s - L_EXP):
                exps(s - L_EXP)
            if ok(s - L_FLIP):
                regroup(s - L_FLIP)
            i_den = s - L_EXP - 1
            den_due = i_den >= 0 and i_den % SUBS == SUBS - 1 and i_den < NT
            if den_due:
                den_add(i_den // SUBS)
            if ph == 0 and 0 < s // SUBS < NBLK:
                edge_max(s // SUBS)
            if ph == 2 and b_prep < NBLK:
                prep_copy(b_prep)
            if ph == 3 and b_prep < NBLK:
                prep_v(b_prep)
            if ph == 1 and 1 < s // SUBS + 1 < NBLK:
                quant_v(s // SUBS + 1)
            if den_due:
                den_recip(i_den // SUBS)
